import numpy as np
import ml_dtypes


def mxq(x, axis, fmt="e4m3"):
    dtype, down = {"e4m3": (ml_dtypes.float8_e4m3fn, 7), "e5m2": (ml_dtypes.float8_e5m2, 14)}[fmt]
    v = np.moveaxis(np.asarray(x, np.float32).astype(ml_dtypes.bfloat16).astype(np.float64), axis, -1)
    blocks = v.reshape(v.shape[:-1] + (-1, 32))
    amax = np.abs(blocks).max(-1, keepdims=True)
    byte = np.maximum(np.where(amax > 0, np.frexp(amax)[1] - 1 + 127, 0) - down, 1)
    scale = np.exp2(byte - 127.0)
    codes = (blocks / scale).astype(np.float32).astype(dtype).astype(np.float64)
    return np.moveaxis((codes * scale).reshape(v.shape), -1, axis)


WIDE = False


def mx_kscale(k):
    if not WIDE:
        return np.ones(k)
    levels = np.array([10, -10, 5, -5, 0])
    a = np.random.permutation(np.resize(levels, k // 512 * 4)).reshape(k // 512, 4)
    idx = np.arange(k)
    return np.exp2(a[idx // 512, idx % 128 // 32])


BF16 = ml_dtypes.bfloat16


def bf(x):
    return np.asarray(x, np.float32).astype(BF16)


def f64(x):
    return np.asarray(x).astype(np.float64)


E2M1 = np.array([0.0, 0.5, 1.0, 1.5, 2.0, 3.0, 4.0, 6.0, -0.0, -0.5, -1.0, -1.5, -2.0, -3.0, -4.0, -6.0])


def pack_weight(w, fmt):
    k, n = w.shape
    w = f64(bf(w)).reshape(k // 32, 32, n)
    amax = np.abs(w).max(1)
    if fmt == "e4m3":
        byte = np.frexp(amax)[1] - 1 + 127 - 7
    else:
        mant, ex = np.frexp(amax / 6.0)
        byte = np.where(mant > 0.5, ex, ex - 1) + 127
    byte = np.clip(np.where(amax > 0, byte, 1), 1, 254)
    scaled = (w * np.exp2(127.0 - byte)[:, None, :]).reshape(k, n).astype(np.float32)
    by_word = np.ascontiguousarray(scaled.reshape(k // 512, 128, 4, n).transpose(0, 1, 3, 2))
    if fmt == "e4m3":
        words = by_word.astype(ml_dtypes.float8_e4m3fn).view(np.uint8)
    else:
        c = by_word.astype(ml_dtypes.float4_e2m1fn).view(np.uint8) & 0xF
        words = c[..., 0::2] | (c[..., 1::2] << 4)
    return np.ascontiguousarray(words), np.ascontiguousarray(byte.astype(np.uint8).reshape(k // 512, 16, n))


def unpack_weight(words, scales, fmt):
    g, p, n, _ = words.shape
    if fmt == "e4m3":
        vals = np.ascontiguousarray(words).view(ml_dtypes.float8_e4m3fn).astype(np.float64)
    else:
        nib = np.empty((g, p, n, 4), np.uint8)
        nib[..., 0::2] = words & 0xF
        nib[..., 1::2] = words >> 4
        vals = E2M1[nib]
    vals = vals * np.repeat(np.exp2(scales.astype(np.float64) - 127.0), 8, axis=1)[..., None]
    return vals.transpose(0, 1, 3, 2).reshape(g * 512, n)

def pack4(w):
    words, scales = pack_weight(w, "e2m1")
    return words.reshape(words.shape[0], 128, -1), scales


def unpack4(words, scales):
    return unpack_weight(words.reshape(words.shape[0], 128, -1, 2), scales, "e2m1")


B, S, D, E = 4, 1024, 512, 2
K = E * D


def setup_inputs():
    s = mx_kscale(K)
    att = bf(np.random.standard_normal((E, B, S, D)) * 0.3 * s.reshape(E, 1, 1, D))
    scene_reps = bf(np.random.standard_normal((B, S, D)))
    wo = np.random.standard_normal((D, K)) * 2.0 / np.sqrt(K) / s[None, :]
    words, scales = pack4(wo.T)
    return {"att": att,
            "scene_reps": scene_reps,
            "Wo_words": words,
            "Wo_scales": scales,
            "bo": bf(np.random.standard_normal(D) * 0.1),
            "gamma": bf(1.0 + np.random.standard_normal(D) * 0.1),
            "beta": bf(np.random.standard_normal(D) * 0.1)}


def reference(att, scene_reps, Wo_words, Wo_scales, bo, gamma, beta):
    cat = np.moveaxis(f64(att), 0, 2).reshape(B, S, K)
    fused = (mxq(cat, 2, "e4m3") @ unpack4(Wo_words, Wo_scales)) + f64(bo)
    y = f64(scene_reps) + fused
    mu = y.mean(-1, keepdims=True)
    var = y.var(-1, keepdims=True)
    return (y - mu) / np.sqrt(var + 1e-5) * f64(gamma) + f64(beta)

@@ -1,0 +1,239 @@
+from contextlib import ExitStack
+
+import concourse.mybir as mybir
+from concourse.masks import make_identity
+
+F32 = mybir.dt.float32
+BF16 = mybir.dt.bfloat16
+I32 = mybir.dt.int32
+U8 = mybir.dt.uint8
+U32 = mybir.dt.uint32
+FP8X4 = mybir.dt.float8_e4m3fn_x4
+FP4X4 = mybir.dt.float4_e2m1fn_x4
+ALU = mybir.AluOpType
+ACT = mybir.ActivationFunctionType
+
+P = 128
+D = 512
+E = 2
+TOKENS = 4096
+EPS = 1e-5
+
+STEP_TILES = 2
+N_STEPS = TOKENS // (P * STEP_TILES)
+WORDS = D // 2
+
+FLOPS = 2 * TOKENS * E * D * D
+
+
+def tile_heterogeneousgraphtransformer_pb_t_kernel(
+    tc, att, scene_reps, Wo_words, Wo_scales, bo, gamma, beta, out
+):
+    nc = tc.nc
+
+    att_steps = att.rearrange("e b s d -> e (b s) d").rearrange(
+        "e (s p i) d -> s p e (i d)", p=P, i=STEP_TILES
+    )
+    res_steps = scene_reps.rearrange("b s d -> (b s) d").rearrange(
+        "(s p i) d -> s p i d", p=P, i=STEP_TILES
+    )
+    out_steps = out.rearrange("b s d -> (b s) d").rearrange(
+        "(s p i) d -> s p i d", p=P, i=STEP_TILES
+    )
+
+    with ExitStack() as stack:
+        stack.enter_context(tc.manual_schedule())
+        const = stack.enter_context(tc.tile_pool(name="const", bufs=1))
+        att_pool = stack.enter_context(tc.tile_pool(name="att", bufs=N_STEPS))
+        res_pool = stack.enter_context(tc.tile_pool(name="res", bufs=N_STEPS))
+        grouped_pool = stack.enter_context(tc.tile_pool(name="grouped", bufs=3))
+        mx_pool = stack.enter_context(tc.tile_pool(name="mx", bufs=4))
+        y_pool = stack.enter_context(tc.tile_pool(name="y", bufs=6))
+        stat_pool = stack.enter_context(tc.tile_pool(name="stat", bufs=4))
+        const_psum = stack.enter_context(tc.psum_pool(name="const_psum", bufs=1))
+        tr_psum = stack.enter_context(tc.psum_pool(name="tr_psum", bufs=2))
+        acc_psum = stack.enter_context(tc.psum_pool(name="acc_psum", bufs=4))
+
+        att_sb = []
+        res_sb = []
+        for s in range(N_STEPS):
+            att_sb.append(att_pool.tile([P, E, STEP_TILES * D], BF16, name="att_sb"))
+            res_sb.append(res_pool.tile([P, STEP_TILES, D], BF16, name="res_sb"))
+
+        nc.sync.dma_start(out=att_sb[0][:], in_=att_steps[0])
+
+        w_words = const.tile([P, E, 2 * D], U8, align_bytes=64)
+        nc.sync.dma_start(
+            out=w_words[:].bitcast(I32),
+            in_=Wo_words.bitcast(I32).rearrange("g p n -> p g n"),
+        )
+        w_scales = const.tile([P, E, D], U8, align_bytes=64)
+        nc.vector.memset(w_scales[:].bitcast(I32), 0)
+        for quadrant in range(4):
+            nc.sync.dma_start(
+                out=w_scales[32 * quadrant : 32 * quadrant + 4].bitcast(I32),
+                in_=Wo_scales.bitcast(I32)[:, 4 * quadrant : 4 * quadrant + 4, :].rearrange(
+                    "g r n -> r g n"
+                ),
+            )
+        nc.sync.dma_start(out=res_sb[0][:], in_=res_steps[0])
+        for s in range(1, N_STEPS):
+            nc.sync.dma_start(out=att_sb[s][:], in_=att_steps[s])
+            nc.sync.dma_start(out=res_sb[s][:], in_=res_steps[s])
+
+        rows = const.tile([P, 3, D], BF16)
+        nc.vector.memset(rows[:], 0.0)
+        ones = const.tile([P, P], BF16)
+        nc.vector.memset(ones[:], 1.0)
+        eps = const.tile([P, 1], F32)
+        nc.vector.memset(eps[:], EPS)
+        for r, vec in enumerate((bo, gamma, beta)):
+            nc.scalar.dma_start(out=rows[0:1, r, :], in_=vec.unsqueeze(0))
+        warm = const.tile([P, 1], F32)
+        nc.scalar.activation(out=warm[:], in_=eps[:], func=ACT.Sqrt)
+
+        ident = const.tile([P, P], F32)
+        make_identity(nc, ident[:])
+
+        bo_ps = acc_psum.tile([P, D], F32, name="acc")
+        gamma_ps = const_psum.tile([P, D], F32)
+        beta_ps = const_psum.tile([P, D], F32)
+        for r, spread in enumerate((bo_ps, gamma_ps, beta_ps)):
+            nc.tensor.matmul(out=spread[:], lhsT=ones[:], rhs=rows[:, r, :], start=True, stop=True)
+        bo_sb = const.tile([P, 1, D], BF16)
+        nc.vector.tensor_copy(out=bo_sb[:, 0, :], in_=bo_ps[:])
+
+        tr_of = {}
+        grouped_of = {}
+        codes_of = {}
+        scales_of = {}
+        acc_of = {}
+        y_of = {}
+        sums_of = {}
+        negmean_of = {}
+        std_of = {}
+
+        def add_bias(s):
+            y_of[s] = y_pool.tile([P, STEP_TILES, D], F32, name="y")
+            nc.gpsimd.tensor_tensor(
+                out=y_of[s][:],
+                in0=res_sb[s][:],
+                in1=bo_sb[:].to_broadcast([P, STEP_TILES, D]),
+                op=ALU.add,
+            )
+
+        def transpose(s):
+            words = att_sb[s][:].bitcast(F32)
+            for i in range(STEP_TILES):
+                tr_of[s, i] = tr_psum.tile([P, E, 2, P], F32, name="tr")
+                for g in range(E):
+                    for u in range(2):
+                        nc.tensor.transpose(
+                            tr_of[s, i][:, g, u, :],
+                            words[:, g, i * WORDS + u : (i + 1) * WORDS : 2],
+                            ident[:],
+                        )
+
+        def regroup(s):
+            grouped_of[s] = grouped_pool.tile(
+                [P, STEP_TILES, E * P * 4], BF16, align_bytes=64, name="grouped"
+            )
+            for i in range(STEP_TILES):
+                nc.scalar.copy(
+                    out=grouped_of[s][:, i, :].bitcast(F32).rearrange(
+                        "p (g r u) -> p g r u", g=E, u=2
+                    ),
+                    in_=tr_of[s, i][:].rearrange("p g u r -> p g r u"),
+                )
+
+        def quantise(s):
+            codes_of[s] = mx_pool.tile([P, STEP_TILES, E, P], U32, align_bytes=64, name="codes")
+            scales_of[s] = mx_pool.tile([P, STEP_TILES, E, P], U8, align_bytes=64, name="scales")
+            nc.vector.quantize_mx(
+                out=codes_of[s][:].rearrange("p i g r -> p (i g r)").bitcast(FP8X4),
+                scales=scales_of[s][:].rearrange("p i g r -> p (i g r)"),
+                in_=grouped_of[s][:].rearrange("p i k -> p (i k)"),
+            )
+
+        def multiply(s):
+            for i in range(STEP_TILES):
+                acc_of[s, i] = acc_psum.tile([P, D], F32, name="acc")
+                for g in range(E):
+                    nc.tensor.matmul_mx(
+                        out=acc_of[s, i][:],
+                        lhsT=codes_of[s][:, i, g, :].bitcast(FP8X4),
+                        lhsT_scale=scales_of[s][:, i, g, :],
+                        rhs=w_words[:, g, :].bitcast(FP4X4),
+                        rhs_scale=w_scales[:, g, :],
+                        start=(g == 0),
+                        stop=(g == E - 1),
+                    )
+
+        def add_product(s):
+            sums_of[s] = stat_pool.tile([P, STEP_TILES], F32, name="sums")
+            for i in range(STEP_TILES):
+                nc.vector.scalar_tensor_tensor(
+                    out=y_of[s][:, i, :],
+                    in0=acc_of[s, i][:],
+                    scalar=0.0,
+                    in1=y_of[s][:, i, :],
+                    op0=ALU.add,
+                    op1=ALU.add,
+                    accum_out=sums_of[s][:, i : i + 1],
+                )
+
+        def statistics(s):
+            negmean_of[s] = stat_pool.tile([P, STEP_TILES], F32, name="negmean")
+            nc.scalar.mul(out=negmean_of[s][:], in_=sums_of[s][:], mul=-1.0 / D)
+            squares = stat_pool.tile([P, STEP_TILES], F32, name="squares")
+            for i in range(STEP_TILES):
+                unused = stat_pool.tile([P, D], BF16, name="unused")
+                nc.scalar.activation(
+                    out=unused[:],
+                    in_=y_of[s][:, i, :],
+                    func=ACT.Square,
+                    bias=negmean_of[s][:, i : i + 1],
+                    scale=1.0,
+                    accum_out=squares[:, i : i + 1],
+                )
+            std_of[s] = stat_pool.tile([P, STEP_TILES], F32, name="std")
+            nc.scalar.activation(
+                out=std_of[s][:], in_=squares[:], func=ACT.Sqrt, bias=eps[:], scale=1.0 / D
+            )
+
+        def normalise_and_store(s):
+            rstd = stat_pool.tile([P, STEP_TILES], F32, name="rstd")
+            nc.vector.reciprocal(out=rstd[:], in_=std_of[s][:])
+            for i in range(STEP_TILES):
+                nc.vector.scalar_tensor_tensor(
+                    out=y_of[s][:, i, :],
+                    in0=y_of[s][:, i, :],
+                    scalar=negmean_of[s][:, i : i + 1],
+                    in1=gamma_ps[:],
+                    op0=ALU.add,
+                    op1=ALU.mult,
+                )
+            for i in range(STEP_TILES):
+                nc.vector.scalar_tensor_tensor(
+                    out=y_of[s][:, i, :],
+                    in0=y_of[s][:, i, :],
+                    scalar=rstd[:, i : i + 1],
+                    in1=beta_ps[:],
+                    op0=ALU.mult,
+                    op1=ALU.add,
+                )
+            nc.sync.dma_start(out=out_steps[s], in_=y_of[s][:])
+
+        def run(stage, s):
+            if 0 <= s < N_STEPS:
+                stage(s)
+
+        for t in range(-4, N_STEPS):
+            run(add_product, t + 1)
+            run(quantise, t + 3)
+            run(add_bias, t + 3)
+            run(transpose, t + 4)
+            run(multiply, t + 3)
+            run(regroup, t + 4)
+            run(statistics, t + 1)
+            run(normalise_and_store, t)

@@ -47,8 +47,9 @@ def tile_heterogeneousgraphtransformer_pb_t_kernel(
         att_pool = stack.enter_context(tc.tile_pool(name="att", bufs=N_STEPS))
         res_pool = stack.enter_context(tc.tile_pool(name="res", bufs=N_STEPS))
         grouped_pool = stack.enter_context(tc.tile_pool(name="grouped", bufs=3))
-        mx_pool = stack.enter_context(tc.tile_pool(name="mx", bufs=4))
-        y_pool = stack.enter_context(tc.tile_pool(name="y", bufs=6))
+        mx_pool = stack.enter_context(tc.tile_pool(name="mx", bufs=3))
+        resb_pool = stack.enter_context(tc.tile_pool(name="resb", bufs=2 * STEP_TILES))
+        y_pool = stack.enter_context(tc.tile_pool(name="y", bufs=4))
         stat_pool = stack.enter_context(tc.tile_pool(name="stat", bufs=4))
         const_psum = stack.enter_context(tc.psum_pool(name="const_psum", bufs=1))
         tr_psum = stack.enter_context(tc.psum_pool(name="tr_psum", bufs=2))
@@ -90,7 +91,7 @@ def tile_heterogeneousgraphtransformer_pb_t_kernel(
         for r, vec in enumerate((bo, gamma, beta)):
             nc.scalar.dma_start(out=rows[0:1, r, :], in_=vec.unsqueeze(0))
         warm = const.tile([P, 1], F32)
-        nc.scalar.activation(out=warm[:], in_=eps[:], func=ACT.Sqrt)
+        nc.scalar.activation(out=warm[:], in_=eps[:], func=ACT.Abs_reciprocal_sqrt)
 
         ident = const.tile([P, P], F32)
         make_identity(nc, ident[:])
@@ -100,27 +101,26 @@ def tile_heterogeneousgraphtransformer_pb_t_kernel(
         beta_ps = const_psum.tile([P, D], F32)
         for r, spread in enumerate((bo_ps, gamma_ps, beta_ps)):
             nc.tensor.matmul(out=spread[:], lhsT=ones[:], rhs=rows[:, r, :], start=True, stop=True)
-        bo_sb = const.tile([P, 1, D], BF16)
-        nc.vector.tensor_copy(out=bo_sb[:, 0, :], in_=bo_ps[:])
+        bo_sb = const.tile([P, D], BF16)
+        nc.vector.tensor_copy(out=bo_sb[:], in_=bo_ps[:])
 
         tr_of = {}
         grouped_of = {}
         codes_of = {}
         scales_of = {}
         acc_of = {}
+        resb_of = {}
         y_of = {}
         sums_of = {}
         negmean_of = {}
-        std_of = {}
+        rstd_of = {}
 
         def add_bias(s):
-            y_of[s] = y_pool.tile([P, STEP_TILES, D], F32, name="y")
-            nc.gpsimd.tensor_tensor(
-                out=y_of[s][:],
-                in0=res_sb[s][:],
-                in1=bo_sb[:].to_broadcast([P, STEP_TILES, D]),
-                op=ALU.add,
-            )
+            for i in range(STEP_TILES):
+                resb_of[s, i] = resb_pool.tile([P, D], F32, name="resb")
+                nc.gpsimd.tensor_tensor(
+                    out=resb_of[s, i][:], in0=res_sb[s][:, i, :], in1=bo_sb[:], op=ALU.add
+                )
 
         def transpose(s):
             words = att_sb[s][:].bitcast(F32)
@@ -170,13 +170,14 @@ def tile_heterogeneousgraphtransformer_pb_t_kernel(
                     )
 
         def add_product(s):
+            y_of[s] = y_pool.tile([P, STEP_TILES, D], F32, name="y")
             sums_of[s] = stat_pool.tile([P, STEP_TILES], F32, name="sums")
             for i in range(STEP_TILES):
                 nc.vector.scalar_tensor_tensor(
                     out=y_of[s][:, i, :],
                     in0=acc_of[s, i][:],
                     scalar=0.0,
-                    in1=y_of[s][:, i, :],
+                    in1=resb_of[s, i][:],
                     op0=ALU.add,
                     op1=ALU.add,
                     accum_out=sums_of[s][:, i : i + 1],
@@ -196,14 +197,16 @@ def tile_heterogeneousgraphtransformer_pb_t_kernel(
                     scale=1.0,
                     accum_out=squares[:, i : i + 1],
                 )
-            std_of[s] = stat_pool.tile([P, STEP_TILES], F32, name="std")
+            rstd_of[s] = stat_pool.tile([P, STEP_TILES], F32, name="rstd")
             nc.scalar.activation(
-                out=std_of[s][:], in_=squares[:], func=ACT.Sqrt, bias=eps[:], scale=1.0 / D
+                out=rstd_of[s][:],
+                in_=squares[:],
+                func=ACT.Abs_reciprocal_sqrt,
+                bias=eps[:],
+                scale=1.0 / D,
             )
 
         def normalise_and_store(s):
-            rstd = stat_pool.tile([P, STEP_TILES], F32, name="rstd")
-            nc.vector.reciprocal(out=rstd[:], in_=std_of[s][:])
             for i in range(STEP_TILES):
                 nc.vector.scalar_tensor_tensor(
                     out=y_of[s][:, i, :],
@@ -217,7 +220,7 @@ def tile_heterogeneousgraphtransformer_pb_t_kernel(
                 nc.vector.scalar_tensor_tensor(
                     out=y_of[s][:, i, :],
                     in0=y_of[s][:, i, :],
-                    scalar=rstd[:, i : i + 1],
+                    scalar=rstd_of[s][:, i : i + 1],
                     in1=beta_ps[:],
                     op0=ALU.mult,
                     op1=ALU.add,
@@ -228,12 +231,12 @@ def tile_heterogeneousgraphtransformer_pb_t_kernel(
             if 0 <= s < N_STEPS:
                 stage(s)
 
-        for t in range(-4, N_STEPS):
+        for t in range(-3, N_STEPS):
+            run(quantise, t + 2)
             run(add_product, t + 1)
-            run(quantise, t + 3)
             run(add_bias, t + 3)
-            run(transpose, t + 4)
-            run(multiply, t + 3)
-            run(regroup, t + 4)
+            run(transpose, t + 3)
+            run(multiply, t + 2)
+            run(regroup, t + 3)
             run(statistics, t + 1)
             run(normalise_and_store, t)

@@ -49,7 +49,7 @@ def tile_heterogeneousgraphtransformer_pb_t_kernel(
         grouped_pool = stack.enter_context(tc.tile_pool(name="grouped", bufs=3))
         mx_pool = stack.enter_context(tc.tile_pool(name="mx", bufs=3))
         resb_pool = stack.enter_context(tc.tile_pool(name="resb", bufs=2 * STEP_TILES))
-        y_pool = stack.enter_context(tc.tile_pool(name="y", bufs=4))
+        y_pool = stack.enter_context(tc.tile_pool(name="y", bufs=N_STEPS // 2))
         stat_pool = stack.enter_context(tc.tile_pool(name="stat", bufs=4))
         const_psum = stack.enter_context(tc.psum_pool(name="const_psum", bufs=1))
         tr_psum = stack.enter_context(tc.psum_pool(name="tr_psum", bufs=2))

@@ -62,6 +62,7 @@ def tile_heterogeneousgraphtransformer_pb_t_kernel(
             res_sb.append(res_pool.tile([P, STEP_TILES, D], BF16, name="res_sb"))
 
         nc.sync.dma_start(out=att_sb[0][:], in_=att_steps[0])
+        nc.sync.dma_start(out=res_sb[0][:], in_=res_steps[0])
 
         w_words = const.tile([P, E, 2 * D], U8, align_bytes=64)
         nc.sync.dma_start(
@@ -77,7 +78,6 @@ def tile_heterogeneousgraphtransformer_pb_t_kernel(
                     "g r n -> r g n"
                 ),
             )
-        nc.sync.dma_start(out=res_sb[0][:], in_=res_steps[0])
         for s in range(1, N_STEPS):
             nc.sync.dma_start(out=att_sb[s][:], in_=att_steps[s])
             nc.sync.dma_start(out=res_sb[s][:], in_=res_steps[s])
@@ -96,13 +96,15 @@ def tile_heterogeneousgraphtransformer_pb_t_kernel(
         ident = const.tile([P, P], F32)
         make_identity(nc, ident[:])
 
+        def spread(r, target):
+            nc.tensor.matmul(out=target[:], lhsT=ones[:], rhs=rows[:, r, :], start=True, stop=True)
+
         bo_ps = acc_psum.tile([P, D], F32, name="acc")
-        gamma_ps = const_psum.tile([P, D], F32)
-        beta_ps = const_psum.tile([P, D], F32)
-        for r, spread in enumerate((bo_ps, gamma_ps, beta_ps)):
-            nc.tensor.matmul(out=spread[:], lhsT=ones[:], rhs=rows[:, r, :], start=True, stop=True)
+        spread(0, bo_ps)
         bo_sb = const.tile([P, D], BF16)
         nc.vector.tensor_copy(out=bo_sb[:], in_=bo_ps[:])
+        gamma_ps = const_psum.tile([P, D], F32)
+        beta_ps = const_psum.tile([P, D], F32)
 
         tr_of = {}
         grouped_of = {}
@@ -225,18 +227,21 @@ def tile_heterogeneousgraphtransformer_pb_t_kernel(
                     op0=ALU.mult,
                     op1=ALU.add,
                 )
-            nc.sync.dma_start(out=out_steps[s], in_=y_of[s][:])
+                nc.sync.dma_start(out=out_steps[s][:, i, :], in_=y_of[s][:, i, :])
 
         def run(stage, s):
             if 0 <= s < N_STEPS:
                 stage(s)
 
+        transpose(0)
+        spread(1, gamma_ps)
+        spread(2, beta_ps)
         for t in range(-3, N_STEPS):
             run(quantise, t + 2)
             run(add_product, t + 1)
             run(add_bias, t + 3)
-            run(transpose, t + 3)
             run(multiply, t + 2)
             run(regroup, t + 3)
             run(statistics, t + 1)
             run(normalise_and_store, t)
+            run(transpose, t + 4)

@@ -48,7 +48,7 @@ def tile_heterogeneousgraphtransformer_pb_t_kernel(
         res_pool = stack.enter_context(tc.tile_pool(name="res", bufs=N_STEPS))
         grouped_pool = stack.enter_context(tc.tile_pool(name="grouped", bufs=3))
         mx_pool = stack.enter_context(tc.tile_pool(name="mx", bufs=3))
-        resb_pool = stack.enter_context(tc.tile_pool(name="resb", bufs=2 * STEP_TILES))
+        resb_pool = stack.enter_context(tc.tile_pool(name="resb", bufs=2))
         y_pool = stack.enter_context(tc.tile_pool(name="y", bufs=N_STEPS // 2))
         stat_pool = stack.enter_context(tc.tile_pool(name="stat", bufs=4))
         const_psum = stack.enter_context(tc.psum_pool(name="const_psum", bufs=1))
@@ -101,8 +101,9 @@ def tile_heterogeneousgraphtransformer_pb_t_kernel(
 
         bo_ps = acc_psum.tile([P, D], F32, name="acc")
         spread(0, bo_ps)
-        bo_sb = const.tile([P, D], BF16)
-        nc.vector.tensor_copy(out=bo_sb[:], in_=bo_ps[:])
+        bo_sb = const.tile([P, STEP_TILES, D], BF16)
+        for i in range(STEP_TILES):
+            nc.vector.tensor_copy(out=bo_sb[:, i, :], in_=bo_ps[:])
         gamma_ps = const_psum.tile([P, D], F32)
         beta_ps = const_psum.tile([P, D], F32)
 
@@ -113,16 +114,12 @@ def tile_heterogeneousgraphtransformer_pb_t_kernel(
         acc_of = {}
         resb_of = {}
         y_of = {}
-        sums_of = {}
         negmean_of = {}
         rstd_of = {}
 
         def add_bias(s):
-            for i in range(STEP_TILES):
-                resb_of[s, i] = resb_pool.tile([P, D], F32, name="resb")
-                nc.gpsimd.tensor_tensor(
-                    out=resb_of[s, i][:], in0=res_sb[s][:, i, :], in1=bo_sb[:], op=ALU.add
-                )
+            resb_of[s] = resb_pool.tile([P, STEP_TILES, D], F32, name="resb")
+            nc.gpsimd.tensor_tensor(out=resb_of[s][:], in0=res_sb[s][:], in1=bo_sb[:], op=ALU.add)
 
         def transpose(s):
             words = att_sb[s][:].bitcast(F32)
@@ -171,25 +168,24 @@ def tile_heterogeneousgraphtransformer_pb_t_kernel(
                         stop=(g == E - 1),
                     )
 
-        def add_product(s):
+        def add_product_and_statistics(s):
             y_of[s] = y_pool.tile([P, STEP_TILES, D], F32, name="y")
-            sums_of[s] = stat_pool.tile([P, STEP_TILES], F32, name="sums")
+            sums = stat_pool.tile([P, STEP_TILES], F32, name="sums")
+            negmean_of[s] = stat_pool.tile([P, STEP_TILES], F32, name="negmean")
+            squares = stat_pool.tile([P, STEP_TILES], F32, name="squares")
             for i in range(STEP_TILES):
                 nc.vector.scalar_tensor_tensor(
                     out=y_of[s][:, i, :],
                     in0=acc_of[s, i][:],
                     scalar=0.0,
-                    in1=resb_of[s, i][:],
+                    in1=resb_of[s][:, i, :],
                     op0=ALU.add,
                     op1=ALU.add,
-                    accum_out=sums_of[s][:, i : i + 1],
+                    accum_out=sums[:, i : i + 1],
                 )
-
-        def statistics(s):
-            negmean_of[s] = stat_pool.tile([P, STEP_TILES], F32, name="negmean")
-            nc.scalar.mul(out=negmean_of[s][:], in_=sums_of[s][:], mul=-1.0 / D)
-            squares = stat_pool.tile([P, STEP_TILES], F32, name="squares")
-            for i in range(STEP_TILES):
+                nc.scalar.mul(
+                    out=negmean_of[s][:, i : i + 1], in_=sums[:, i : i + 1], mul=-1.0 / D
+                )
                 unused = stat_pool.tile([P, D], BF16, name="unused")
                 nc.scalar.activation(
                     out=unused[:],
@@ -238,10 +234,9 @@ def tile_heterogeneousgraphtransformer_pb_t_kernel(
         spread(2, beta_ps)
         for t in range(-3, N_STEPS):
             run(quantise, t + 2)
-            run(add_product, t + 1)
-            run(add_bias, t + 3)
+            run(add_bias, t + 2)
             run(multiply, t + 2)
             run(regroup, t + 3)
-            run(statistics, t + 1)
             run(normalise_and_store, t)
             run(transpose, t + 4)
+            run(add_product_and_statistics, t + 1)

@@ -22,6 +22,8 @@ EPS = 1e-5
 STEP_TILES = 2
 N_STEPS = TOKENS // (P * STEP_TILES)
 WORDS = D // 2
+GP_COLS = 128
+VE_COLS = D - GP_COLS
 
 FLOPS = 2 * TOKENS * E * D * D
 
@@ -106,6 +108,7 @@ def tile_heterogeneousgraphtransformer_pb_t_kernel(
             nc.vector.tensor_copy(out=bo_sb[:, i, :], in_=bo_ps[:])
         gamma_ps = const_psum.tile([P, D], F32)
         beta_ps = const_psum.tile([P, D], F32)
+        beta_sb = const.tile([P, STEP_TILES, GP_COLS], F32)
 
         tr_of = {}
         grouped_of = {}
@@ -204,7 +207,7 @@ def tile_heterogeneousgraphtransformer_pb_t_kernel(
                 scale=1.0 / D,
             )
 
-        def normalise_and_store(s):
+        def centre(s):
             for i in range(STEP_TILES):
                 nc.vector.scalar_tensor_tensor(
                     out=y_of[s][:, i, :],
@@ -215,14 +218,27 @@ def tile_heterogeneousgraphtransformer_pb_t_kernel(
                     op1=ALU.mult,
                 )
             for i in range(STEP_TILES):
+                nc.scalar.activation(
+                    out=y_of[s][:, i, VE_COLS:],
+                    in_=y_of[s][:, i, VE_COLS:],
+                    func=ACT.Copy,
+                    scale=rstd_of[s][:, i : i + 1],
+                )
+
+        def finish_and_store(s):
+            for i in range(STEP_TILES):
                 nc.vector.scalar_tensor_tensor(
-                    out=y_of[s][:, i, :],
-                    in0=y_of[s][:, i, :],
+                    out=y_of[s][:, i, :VE_COLS],
+                    in0=y_of[s][:, i, :VE_COLS],
                     scalar=rstd_of[s][:, i : i + 1],
-                    in1=beta_ps[:],
+                    in1=beta_ps[:, :VE_COLS],
                     op0=ALU.mult,
                     op1=ALU.add,
                 )
+            nc.gpsimd.tensor_tensor(
+                out=y_of[s][:, :, VE_COLS:], in0=y_of[s][:, :, VE_COLS:], in1=beta_sb[:], op=ALU.add
+            )
+            for i in range(STEP_TILES):
                 nc.sync.dma_start(out=out_steps[s][:, i, :], in_=y_of[s][:, i, :])
 
         def run(stage, s):
@@ -232,11 +248,15 @@ def tile_heterogeneousgraphtransformer_pb_t_kernel(
         transpose(0)
         spread(1, gamma_ps)
         spread(2, beta_ps)
-        for t in range(-3, N_STEPS):
+        for t in range(-3, N_STEPS + 1):
             run(quantise, t + 2)
+            if t == -2:
+                for i in range(STEP_TILES):
+                    nc.vector.tensor_copy(out=beta_sb[:, i, :], in_=beta_ps[:, VE_COLS:])
             run(add_bias, t + 2)
             run(multiply, t + 2)
+            run(finish_and_store, t - 1)
             run(regroup, t + 3)
-            run(normalise_and_store, t)
+            run(centre, t)
             run(transpose, t + 4)
             run(add_product_and_statistics, t + 1)

@@ -22,7 +22,7 @@ EPS = 1e-5
 STEP_TILES = 2
 N_STEPS = TOKENS // (P * STEP_TILES)
 WORDS = D // 2
-GP_COLS = 128
+GP_COLS = 96
 VE_COLS = D - GP_COLS
 
 FLOPS = 2 * TOKENS * E * D * D
@@ -48,9 +48,8 @@ def tile_heterogeneousgraphtransformer_pb_t_kernel(
         const = stack.enter_context(tc.tile_pool(name="const", bufs=1))
         att_pool = stack.enter_context(tc.tile_pool(name="att", bufs=N_STEPS))
         res_pool = stack.enter_context(tc.tile_pool(name="res", bufs=N_STEPS))
-        grouped_pool = stack.enter_context(tc.tile_pool(name="grouped", bufs=3))
+        slot_pool = stack.enter_context(tc.tile_pool(name="slot", bufs=3))
         mx_pool = stack.enter_context(tc.tile_pool(name="mx", bufs=3))
-        resb_pool = stack.enter_context(tc.tile_pool(name="resb", bufs=2))
         y_pool = stack.enter_context(tc.tile_pool(name="y", bufs=N_STEPS // 2))
         stat_pool = stack.enter_context(tc.tile_pool(name="stat", bufs=4))
         const_psum = stack.enter_context(tc.psum_pool(name="const_psum", bufs=1))
@@ -121,8 +120,20 @@ def tile_heterogeneousgraphtransformer_pb_t_kernel(
         rstd_of = {}
 
         def add_bias(s):
-            resb_of[s] = resb_pool.tile([P, STEP_TILES, D], F32, name="resb")
+            resb_of[s] = slot_pool.tile([P, STEP_TILES, D], F32, align_bytes=64, name="slot")
             nc.gpsimd.tensor_tensor(out=resb_of[s][:], in0=res_sb[s][:], in1=bo_sb[:], op=ALU.add)
+
+        def add_bias_on_vector(s):
+            resb_of[s] = slot_pool.tile([P, STEP_TILES, D], F32, align_bytes=64, name="slot")
+            for i in range(STEP_TILES):
+                nc.vector.tensor_tensor(
+                    out=resb_of[s][:, i, :], in0=res_sb[s][:, i, :], in1=bo_ps[:], op=ALU.add
+                )
+
+        def take_grouped(s):
+            grouped_of[s] = slot_pool.tile(
+                [P, STEP_TILES, E * P * 4], BF16, align_bytes=64, name="slot"
+            )
 
         def transpose(s):
             words = att_sb[s][:].bitcast(F32)
@@ -137,9 +148,6 @@ def tile_heterogeneousgraphtransformer_pb_t_kernel(
                         )
 
         def regroup(s):
-            grouped_of[s] = grouped_pool.tile(
-                [P, STEP_TILES, E * P * 4], BF16, align_bytes=64, name="grouped"
-            )
             for i in range(STEP_TILES):
                 nc.scalar.copy(
                     out=grouped_of[s][:, i, :].bitcast(F32).rearrange(
@@ -249,11 +257,15 @@ def tile_heterogeneousgraphtransformer_pb_t_kernel(
         spread(1, gamma_ps)
         spread(2, beta_ps)
         for t in range(-3, N_STEPS + 1):
+            run(take_grouped, t + 3)
+            if t == -2:
+                add_bias_on_vector(0)
             run(quantise, t + 2)
             if t == -2:
                 for i in range(STEP_TILES):
                     nc.vector.tensor_copy(out=beta_sb[:, i, :], in_=beta_ps[:, VE_COLS:])
-            run(add_bias, t + 2)
+            else:
+                run(add_bias, t + 2)
             run(multiply, t + 2)
             run(finish_and_store, t - 1)
             run(regroup, t + 3)

@@ -120,11 +120,13 @@ def tile_heterogeneousgraphtransformer_pb_t_kernel(
         rstd_of = {}
 
         def add_bias(s):
-            resb_of[s] = slot_pool.tile([P, STEP_TILES, D], F32, align_bytes=64, name="slot")
+            take_resb(s)
             nc.gpsimd.tensor_tensor(out=resb_of[s][:], in0=res_sb[s][:], in1=bo_sb[:], op=ALU.add)
 
-        def add_bias_on_vector(s):
+        def take_resb(s):
             resb_of[s] = slot_pool.tile([P, STEP_TILES, D], F32, align_bytes=64, name="slot")
+
+        def add_bias_on_vector(s):
             for i in range(STEP_TILES):
                 nc.vector.tensor_tensor(
                     out=resb_of[s][:, i, :], in0=res_sb[s][:, i, :], in1=bo_ps[:], op=ALU.add
@@ -256,19 +258,20 @@ def tile_heterogeneousgraphtransformer_pb_t_kernel(
         transpose(0)
         spread(1, gamma_ps)
         spread(2, beta_ps)
-        for t in range(-3, N_STEPS + 1):
-            run(take_grouped, t + 3)
+        for t in range(-2, N_STEPS + 1):
+            run(take_grouped, t + 2)
+            run(quantise, t + 1)
             if t == -2:
-                add_bias_on_vector(0)
-            run(quantise, t + 2)
-            if t == -2:
-                for i in range(STEP_TILES):
-                    nc.vector.tensor_copy(out=beta_sb[:, i, :], in_=beta_ps[:, VE_COLS:])
+                take_resb(0)
             else:
                 run(add_bias, t + 2)
-            run(multiply, t + 2)
+            if t == -1:
+                add_bias_on_vector(0)
+                for i in range(STEP_TILES):
+                    nc.vector.tensor_copy(out=beta_sb[:, i, :], in_=beta_ps[:, VE_COLS:])
+            run(multiply, t + 1)
             run(finish_and_store, t - 1)
-            run(regroup, t + 3)
+            run(regroup, t + 2)
             run(centre, t)
-            run(transpose, t + 4)
+            run(transpose, t + 3)
             run(add_product_and_statistics, t + 1)

@@ -62,8 +62,10 @@ def tile_heterogeneousgraphtransformer_pb_t_kernel(
             att_sb.append(att_pool.tile([P, E, STEP_TILES * D], BF16, name="att_sb"))
             res_sb.append(res_pool.tile([P, STEP_TILES, D], BF16, name="res_sb"))
 
-        nc.sync.dma_start(out=att_sb[0][:], in_=att_steps[0])
-        nc.sync.dma_start(out=res_sb[0][:], in_=res_steps[0])
+        for i in range(STEP_TILES):
+            nc.sync.dma_start(
+                out=att_sb[0][:, :, i * D : (i + 1) * D], in_=att_steps[0][:, :, i * D : (i + 1) * D]
+            )
 
         w_words = const.tile([P, E, 2 * D], U8, align_bytes=64)
         nc.sync.dma_start(
@@ -79,6 +81,7 @@ def tile_heterogeneousgraphtransformer_pb_t_kernel(
                     "g r n -> r g n"
                 ),
             )
+        nc.sync.dma_start(out=res_sb[0][:], in_=res_steps[0])
         for s in range(1, N_STEPS):
             nc.sync.dma_start(out=att_sb[s][:], in_=att_steps[s])
             nc.sync.dma_start(out=res_sb[s][:], in_=res_steps[s])
@@ -96,15 +99,14 @@ def tile_heterogeneousgraphtransformer_pb_t_kernel(
 
         ident = const.tile([P, P], F32)
         make_identity(nc, ident[:])
+        zeros = const.tile([P, D], BF16)
+        nc.vector.memset(zeros[:], 0.0)
 
         def spread(r, target):
             nc.tensor.matmul(out=target[:], lhsT=ones[:], rhs=rows[:, r, :], start=True, stop=True)
 
         bo_ps = acc_psum.tile([P, D], F32, name="acc")
-        spread(0, bo_ps)
         bo_sb = const.tile([P, STEP_TILES, D], BF16)
-        for i in range(STEP_TILES):
-            nc.vector.tensor_copy(out=bo_sb[:, i, :], in_=bo_ps[:])
         gamma_ps = const_psum.tile([P, D], F32)
         beta_ps = const_psum.tile([P, D], F32)
         beta_sb = const.tile([P, STEP_TILES, GP_COLS], F32)
@@ -166,6 +168,16 @@ def tile_heterogeneousgraphtransformer_pb_t_kernel(
                 scales=scales_of[s][:].rearrange("p i g r -> p (i g r)"),
                 in_=grouped_of[s][:].rearrange("p i k -> p (i k)"),
             )
+
+        def quantise_by_tiles(s):
+            codes_of[s] = mx_pool.tile([P, STEP_TILES, E, P], U32, align_bytes=64, name="codes")
+            scales_of[s] = mx_pool.tile([P, STEP_TILES, E, P], U8, align_bytes=64, name="scales")
+            for i in range(STEP_TILES):
+                nc.vector.quantize_mx(
+                    out=codes_of[s][:, i].rearrange("p g r -> p (g r)").bitcast(FP8X4),
+                    scales=scales_of[s][:, i].rearrange("p g r -> p (g r)"),
+                    in_=grouped_of[s][:, i, :],
+                )
 
         def multiply(s):
             for i in range(STEP_TILES):
@@ -255,20 +267,32 @@ def tile_heterogeneousgraphtransformer_pb_t_kernel(
             if 0 <= s < N_STEPS:
                 stage(s)
 
+        for warm_up in range(2):
+            nc.tensor.matmul(out=gamma_ps[:], lhsT=ones[:], rhs=zeros[:], start=True, stop=True)
         transpose(0)
+        spread(0, bo_ps)
+        take_grouped(0)
+        take_resb(0)
+        regroup(0)
+        quantise_by_tiles(0)
+        for i in range(STEP_TILES):
+            nc.vector.tensor_copy(out=bo_sb[:, i, :], in_=bo_ps[:])
+        add_bias_on_vector(0)
+        multiply(0)
+        transpose(1)
         spread(1, gamma_ps)
         spread(2, beta_ps)
-        for t in range(-2, N_STEPS + 1):
+        take_grouped(1)
+        add_bias(1)
+        regroup(1)
+        for i in range(STEP_TILES):
+            nc.scalar.copy(out=beta_sb[:, i, :], in_=beta_ps[:, VE_COLS:])
+        transpose(2)
+        add_product_and_statistics(0)
+        for t in range(N_STEPS + 1):
             run(take_grouped, t + 2)
             run(quantise, t + 1)
-            if t == -2:
-                take_resb(0)
-            else:
-                run(add_bias, t + 2)
-            if t == -1:
-                add_bias_on_vector(0)
-                for i in range(STEP_TILES):
-                    nc.vector.tensor_copy(out=beta_sb[:, i, :], in_=beta_ps[:, VE_COLS:])
+            run(add_bias, t + 2)
             run(multiply, t + 1)
             run(finish_and_store, t - 1)
             run(regroup, t + 2)

@@ -22,7 +22,7 @@ EPS = 1e-5
 STEP_TILES = 2
 N_STEPS = TOKENS // (P * STEP_TILES)
 WORDS = D // 2
-GP_COLS = 96
+GP_COLS = 128
 VE_COLS = D - GP_COLS
 
 FLOPS = 2 * TOKENS * E * D * D
@@ -106,10 +106,11 @@ def tile_heterogeneousgraphtransformer_pb_t_kernel(
             nc.tensor.matmul(out=target[:], lhsT=ones[:], rhs=rows[:, r, :], start=True, stop=True)
 
         bo_ps = acc_psum.tile([P, D], F32, name="acc")
-        bo_sb = const.tile([P, STEP_TILES, D], BF16)
+        bo_ps_for_copy = acc_psum.tile([P, D], F32, name="acc")
+        bo_sb = const.tile([P, D], BF16)
         gamma_ps = const_psum.tile([P, D], F32)
         beta_ps = const_psum.tile([P, D], F32)
-        beta_sb = const.tile([P, STEP_TILES, GP_COLS], F32)
+        beta_sb = const.tile([P, GP_COLS], F32)
 
         tr_of = {}
         grouped_of = {}
@@ -123,7 +124,12 @@ def tile_heterogeneousgraphtransformer_pb_t_kernel(
 
         def add_bias(s):
             take_resb(s)
-            nc.gpsimd.tensor_tensor(out=resb_of[s][:], in0=res_sb[s][:], in1=bo_sb[:], op=ALU.add)
+            nc.gpsimd.tensor_tensor(
+                out=resb_of[s][:],
+                in0=res_sb[s][:],
+                in1=bo_sb[:].unsqueeze(1).to_broadcast([P, STEP_TILES, D]),
+                op=ALU.add,
+            )
 
         def take_resb(s):
             resb_of[s] = slot_pool.tile([P, STEP_TILES, D], F32, align_bytes=64, name="slot")
@@ -208,17 +214,17 @@ def tile_heterogeneousgraphtransformer_pb_t_kernel(
                     op1=ALU.add,
                     accum_out=sums[:, i : i + 1],
                 )
-                nc.scalar.mul(
-                    out=negmean_of[s][:, i : i + 1], in_=sums[:, i : i + 1], mul=-1.0 / D
-                )
                 unused = stat_pool.tile([P, D], BF16, name="unused")
                 nc.scalar.activation(
                     out=unused[:],
                     in_=y_of[s][:, i, :],
                     func=ACT.Square,
-                    bias=negmean_of[s][:, i : i + 1],
-                    scale=1.0,
+                    bias=sums[:, i : i + 1],
+                    scale=-1.0 * D,
                     accum_out=squares[:, i : i + 1],
+                )
+                nc.scalar.mul(
+                    out=negmean_of[s][:, i : i + 1], in_=sums[:, i : i + 1], mul=-1.0 / D
                 )
             rstd_of[s] = stat_pool.tile([P, STEP_TILES], F32, name="rstd")
             nc.scalar.activation(
@@ -226,7 +232,7 @@ def tile_heterogeneousgraphtransformer_pb_t_kernel(
                 in_=squares[:],
                 func=ACT.Abs_reciprocal_sqrt,
                 bias=eps[:],
-                scale=1.0 / D,
+                scale=1.0 / (D * D * D),
             )
 
         def centre(s):
@@ -239,6 +245,8 @@ def tile_heterogeneousgraphtransformer_pb_t_kernel(
                     op0=ALU.add,
                     op1=ALU.mult,
                 )
+            if s == N_STEPS - 1:
+                return
             for i in range(STEP_TILES):
                 nc.scalar.activation(
                     out=y_of[s][:, i, VE_COLS:],
@@ -248,17 +256,26 @@ def tile_heterogeneousgraphtransformer_pb_t_kernel(
                 )
 
         def finish_and_store(s):
+            last = s == N_STEPS - 1
+            cols = D if last else VE_COLS
             for i in range(STEP_TILES):
                 nc.vector.scalar_tensor_tensor(
-                    out=y_of[s][:, i, :VE_COLS],
-                    in0=y_of[s][:, i, :VE_COLS],
+                    out=y_of[s][:, i, :cols],
+                    in0=y_of[s][:, i, :cols],
                     scalar=rstd_of[s][:, i : i + 1],
-                    in1=beta_ps[:, :VE_COLS],
+                    in1=beta_ps[:, :cols],
                     op0=ALU.mult,
                     op1=ALU.add,
                 )
+                if last:
+                    nc.sync.dma_start(out=out_steps[s][:, i, :], in_=y_of[s][:, i, :])
+            if last:
+                return
             nc.gpsimd.tensor_tensor(
-                out=y_of[s][:, :, VE_COLS:], in0=y_of[s][:, :, VE_COLS:], in1=beta_sb[:], op=ALU.add
+                out=y_of[s][:, :, VE_COLS:],
+                in0=y_of[s][:, :, VE_COLS:],
+                in1=beta_sb[:].unsqueeze(1).to_broadcast([P, STEP_TILES, GP_COLS]),
+                op=ALU.add,
             )
             for i in range(STEP_TILES):
                 nc.sync.dma_start(out=out_steps[s][:, i, :], in_=y_of[s][:, i, :])
@@ -271,12 +288,12 @@ def tile_heterogeneousgraphtransformer_pb_t_kernel(
             nc.tensor.matmul(out=gamma_ps[:], lhsT=ones[:], rhs=zeros[:], start=True, stop=True)
         transpose(0)
         spread(0, bo_ps)
+        spread(0, bo_ps_for_copy)
         take_grouped(0)
         take_resb(0)
         regroup(0)
+        nc.scalar.copy(out=bo_sb[:], in_=bo_ps_for_copy[:])
         quantise_by_tiles(0)
-        for i in range(STEP_TILES):
-            nc.vector.tensor_copy(out=bo_sb[:, i, :], in_=bo_ps[:])
         add_bias_on_vector(0)
         multiply(0)
         transpose(1)
@@ -285,8 +302,7 @@ def tile_heterogeneousgraphtransformer_pb_t_kernel(
         take_grouped(1)
         add_bias(1)
         regroup(1)
-        for i in range(STEP_TILES):
-            nc.scalar.copy(out=beta_sb[:, i, :], in_=beta_ps[:, VE_COLS:])
+        nc.scalar.copy(out=beta_sb[:], in_=beta_ps[:, VE_COLS:])
         transpose(2)
         add_product_and_statistics(0)
         for t in range(N_STEPS + 1):

from contextlib import ExitStack

import concourse.mybir as mybir
from concourse.masks import make_identity

F32 = mybir.dt.float32
BF16 = mybir.dt.bfloat16
I32 = mybir.dt.int32
U8 = mybir.dt.uint8
U32 = mybir.dt.uint32
FP8X4 = mybir.dt.float8_e4m3fn_x4
FP4X4 = mybir.dt.float4_e2m1fn_x4
ALU = mybir.AluOpType
ACT = mybir.ActivationFunctionType

P = 128
D = 512
E = 2
TOKENS = 4096
EPS = 1e-5

STEP_TILES = 2
N_STEPS = TOKENS // (P * STEP_TILES)
WORDS = D // 2
GP_COLS = 128
VE_COLS = D - GP_COLS

FLOPS = 2 * TOKENS * E * D * D


def tile_heterogeneousgraphtransformer_pb_t_kernel(
    tc, att, scene_reps, Wo_words, Wo_scales, bo, gamma, beta, out
):
    nc = tc.nc

    att_steps = att.rearrange("e b s d -> e (b s) d").rearrange(
        "e (s p i) d -> s p e (i d)", p=P, i=STEP_TILES
    )
    res_steps = scene_reps.rearrange("b s d -> (b s) d").rearrange(
        "(s p i) d -> s p i d", p=P, i=STEP_TILES
    )
    out_steps = out.rearrange("b s d -> (b s) d").rearrange(
        "(s p i) d -> s p i d", p=P, i=STEP_TILES
    )

    with ExitStack() as stack:
        stack.enter_context(tc.manual_schedule())
        const = stack.enter_context(tc.tile_pool(name="const", bufs=1))
        att_pool = stack.enter_context(tc.tile_pool(name="att", bufs=N_STEPS))
        res_pool = stack.enter_context(tc.tile_pool(name="res", bufs=N_STEPS))
        slot_pool = stack.enter_context(tc.tile_pool(name="slot", bufs=3))
        mx_pool = stack.enter_context(tc.tile_pool(name="mx", bufs=3))
        y_pool = stack.enter_context(tc.tile_pool(name="y", bufs=N_STEPS // 2))
        stat_pool = stack.enter_context(tc.tile_pool(name="stat", bufs=4))
        const_psum = stack.enter_context(tc.psum_pool(name="const_psum", bufs=1))
        tr_psum = stack.enter_context(tc.psum_pool(name="tr_psum", bufs=2))
        acc_psum = stack.enter_context(tc.psum_pool(name="acc_psum", bufs=4))

        att_sb = []
        res_sb = []
        for s in range(N_STEPS):
            att_sb.append(att_pool.tile([P, E, STEP_TILES * D], BF16, name="att_sb"))
            res_sb.append(res_pool.tile([P, STEP_TILES, D], BF16, name="res_sb"))

        for i in range(STEP_TILES):
            nc.sync.dma_start(
                out=att_sb[0][:, :, i * D : (i + 1) * D], in_=att_steps[0][:, :, i * D : (i + 1) * D]
            )

        w_words = const.tile([P, E, 2 * D], U8, align_bytes=64)
        nc.sync.dma_start(
            out=w_words[:].bitcast(I32),
            in_=Wo_words.bitcast(I32).rearrange("g p n -> p g n"),
        )
        w_scales = const.tile([P, E, D], U8, align_bytes=64)
        nc.vector.memset(w_scales[:].bitcast(I32), 0)
        for quadrant in range(4):
            nc.sync.dma_start(
                out=w_scales[32 * quadrant : 32 * quadrant + 4].bitcast(I32),
                in_=Wo_scales.bitcast(I32)[:, 4 * quadrant : 4 * quadrant + 4, :].rearrange(
                    "g r n -> r g n"
                ),
            )
        nc.sync.dma_start(out=res_sb[0][:], in_=res_steps[0])
        for s in range(1, N_STEPS):
            nc.sync.dma_start(out=att_sb[s][:], in_=att_steps[s])
            nc.sync.dma_start(out=res_sb[s][:], in_=res_steps[s])

        rows = const.tile([P, 3, D], BF16)
        nc.vector.memset(rows[:], 0.0)
        ones = const.tile([P, P], BF16)
        nc.vector.memset(ones[:], 1.0)
        eps = const.tile([P, 1], F32)
        nc.vector.memset(eps[:], EPS)
        for r, vec in enumerate((bo, gamma, beta)):
            nc.scalar.dma_start(out=rows[0:1, r, :], in_=vec.unsqueeze(0))
        warm = const.tile([P, 1], F32)
        nc.scalar.activation(out=warm[:], in_=eps[:], func=ACT.Abs_reciprocal_sqrt)

        ident = const.tile([P, P], F32)
        make_identity(nc, ident[:])
        zeros = const.tile([P, D], BF16)
        nc.vector.memset(zeros[:], 0.0)

        def spread(r, target):
            nc.tensor.matmul(out=target[:], lhsT=ones[:], rhs=rows[:, r, :], start=True, stop=True)

        bo_ps = acc_psum.tile([P, D], F32, name="acc")
        bo_ps_for_copy = acc_psum.tile([P, D], F32, name="acc")
        bo_sb = const.tile([P, D], BF16)
        gamma_ps = const_psum.tile([P, D], F32)
        beta_ps = const_psum.tile([P, D], F32)
        beta_sb = const.tile([P, GP_COLS], F32)

        tr_of = {}
        grouped_of = {}
        codes_of = {}
        scales_of = {}
        acc_of = {}
        resb_of = {}
        y_of = {}
        negmean_of = {}
        rstd_of = {}

        def add_bias(s):
            take_resb(s)
            nc.gpsimd.tensor_tensor(
                out=resb_of[s][:],
                in0=res_sb[s][:],
                in1=bo_sb[:].unsqueeze(1).to_broadcast([P, STEP_TILES, D]),
                op=ALU.add,
            )

        def take_resb(s):
            resb_of[s] = slot_pool.tile([P, STEP_TILES, D], F32, align_bytes=64, name="slot")

        def add_bias_on_vector(s):
            for i in range(STEP_TILES):
                nc.vector.tensor_tensor(
                    out=resb_of[s][:, i, :], in0=res_sb[s][:, i, :], in1=bo_ps[:], op=ALU.add
                )

        def take_grouped(s):
            grouped_of[s] = slot_pool.tile(
                [P, STEP_TILES, E * P * 4], BF16, align_bytes=64, name="slot"
            )

        def transpose(s):
            words = att_sb[s][:].bitcast(F32)
            for i in range(STEP_TILES):
                tr_of[s, i] = tr_psum.tile([P, E, 2, P], F32, name="tr")
                for g in range(E):
                    for u in range(2):
                        nc.tensor.transpose(
                            tr_of[s, i][:, g, u, :],
                            words[:, g, i * WORDS + u : (i + 1) * WORDS : 2],
                            ident[:],
                        )

        def regroup(s):
            for i in range(STEP_TILES):
                nc.scalar.copy(
                    out=grouped_of[s][:, i, :].bitcast(F32).rearrange(
                        "p (g r u) -> p g r u", g=E, u=2
                    ),
                    in_=tr_of[s, i][:].rearrange("p g u r -> p g r u"),
                )

        def quantise(s):
            codes_of[s] = mx_pool.tile([P, STEP_TILES, E, P], U32, align_bytes=64, name="codes")
            scales_of[s] = mx_pool.tile([P, STEP_TILES, E, P], U8, align_bytes=64, name="scales")
            nc.vector.quantize_mx(
                out=codes_of[s][:].rearrange("p i g r -> p (i g r)").bitcast(FP8X4),
                scales=scales_of[s][:].rearrange("p i g r -> p (i g r)"),
                in_=grouped_of[s][:].rearrange("p i k -> p (i k)"),
            )

        def quantise_by_tiles(s):
            codes_of[s] = mx_pool.tile([P, STEP_TILES, E, P], U32, align_bytes=64, name="codes")
            scales_of[s] = mx_pool.tile([P, STEP_TILES, E, P], U8, align_bytes=64, name="scales")
            for i in range(STEP_TILES):
                nc.vector.quantize_mx(
                    out=codes_of[s][:, i].rearrange("p g r -> p (g r)").bitcast(FP8X4),
                    scales=scales_of[s][:, i].rearrange("p g r -> p (g r)"),
                    in_=grouped_of[s][:, i, :],
                )

        def multiply(s):
            for i in range(STEP_TILES):
                acc_of[s, i] = acc_psum.tile([P, D], F32, name="acc")
                for g in range(E):
                    nc.tensor.matmul_mx(
                        out=acc_of[s, i][:],
                        lhsT=codes_of[s][:, i, g, :].bitcast(FP8X4),
                        lhsT_scale=scales_of[s][:, i, g, :],
                        rhs=w_words[:, g, :].bitcast(FP4X4),
                        rhs_scale=w_scales[:, g, :],
                        start=(g == 0),
                        stop=(g == E - 1),
                    )

        def add_product_and_statistics(s):
            y_of[s] = y_pool.tile([P, STEP_TILES, D], F32, name="y")
            sums = stat_pool.tile([P, STEP_TILES], F32, name="sums")
            negmean_of[s] = stat_pool.tile([P, STEP_TILES], F32, name="negmean")
            squares = stat_pool.tile([P, STEP_TILES], F32, name="squares")
            for i in range(STEP_TILES):
                nc.vector.scalar_tensor_tensor(
                    out=y_of[s][:, i, :],
                    in0=acc_of[s, i][:],
                    scalar=0.0,
                    in1=resb_of[s][:, i, :],
                    op0=ALU.add,
                    op1=ALU.add,
                    accum_out=sums[:, i : i + 1],
                )
                unused = stat_pool.tile([P, D], BF16, name="unused")
                nc.scalar.activation(
                    out=unused[:],
                    in_=y_of[s][:, i, :],
                    func=ACT.Square,
                    bias=sums[:, i : i + 1],
                    scale=-1.0 * D,
                    accum_out=squares[:, i : i + 1],
                )
                nc.scalar.mul(
                    out=negmean_of[s][:, i : i + 1], in_=sums[:, i : i + 1], mul=-1.0 / D
                )
            rstd_of[s] = stat_pool.tile([P, STEP_TILES], F32, name="rstd")
            nc.scalar.activation(
                out=rstd_of[s][:],
                in_=squares[:],
                func=ACT.Abs_reciprocal_sqrt,
                bias=eps[:],
                scale=1.0 / (D * D * D),
            )

        def centre(s):
            for i in range(STEP_TILES):
                nc.vector.scalar_tensor_tensor(
                    out=y_of[s][:, i, :],
                    in0=y_of[s][:, i, :],
                    scalar=negmean_of[s][:, i : i + 1],
                    in1=gamma_ps[:],
                    op0=ALU.add,
                    op1=ALU.mult,
                )
            if s == N_STEPS - 1:
                return
            for i in range(STEP_TILES):
                nc.scalar.activation(
                    out=y_of[s][:, i, VE_COLS:],
                    in_=y_of[s][:, i, VE_COLS:],
                    func=ACT.Copy,
                    scale=rstd_of[s][:, i : i + 1],
                )

        def finish_and_store(s):
            last = s == N_STEPS - 1
            cols = D if last else VE_COLS
            for i in range(STEP_TILES):
                nc.vector.scalar_tensor_tensor(
                    out=y_of[s][:, i, :cols],
                    in0=y_of[s][:, i, :cols],
                    scalar=rstd_of[s][:, i : i + 1],
                    in1=beta_ps[:, :cols],
                    op0=ALU.mult,
                    op1=ALU.add,
                )
                if last:
                    nc.sync.dma_start(out=out_steps[s][:, i, :], in_=y_of[s][:, i, :])
            if last:
                return
            nc.gpsimd.tensor_tensor(
                out=y_of[s][:, :, VE_COLS:],
                in0=y_of[s][:, :, VE_COLS:],
                in1=beta_sb[:].unsqueeze(1).to_broadcast([P, STEP_TILES, GP_COLS]),
                op=ALU.add,
            )
            for i in range(STEP_TILES):
                nc.sync.dma_start(out=out_steps[s][:, i, :], in_=y_of[s][:, i, :])

        def run(stage, s):
            if 0 <= s < N_STEPS:
                stage(s)

        for warm_up in range(2):
            nc.tensor.matmul(out=gamma_ps[:], lhsT=ones[:], rhs=zeros[:], start=True, stop=True)
        transpose(0)
        spread(0, bo_ps)
        spread(0, bo_ps_for_copy)
        take_grouped(0)
        take_resb(0)
        regroup(0)
        nc.scalar.copy(out=bo_sb[:], in_=bo_ps_for_copy[:])
        quantise_by_tiles(0)
        add_bias_on_vector(0)
        multiply(0)
        transpose(1)
        spread(1, gamma_ps)
        spread(2, beta_ps)
        take_grouped(1)
        add_bias(1)
        regroup(1)
        nc.scalar.copy(out=beta_sb[:], in_=beta_ps[:, VE_COLS:])
        transpose(2)
        add_product_and_statistics(0)
        for t in range(N_STEPS + 1):
            run(take_grouped, t + 2)
            run(quantise, t + 1)
            run(add_bias, t + 2)
            run(multiply, t + 1)
            run(finish_and_store, t - 1)
            run(regroup, t + 2)
            run(centre, t)
            run(transpose, t + 3)
            run(add_product_and_statistics, t + 1)
